import numpy as np
import ml_dtypes


def mxq(x, axis, fmt="e4m3"):
    dtype, down = {"e4m3": (ml_dtypes.float8_e4m3fn, 7), "e5m2": (ml_dtypes.float8_e5m2, 14)}[fmt]
    v = np.moveaxis(np.asarray(x, np.float32).astype(ml_dtypes.bfloat16).astype(np.float64), axis, -1)
    blocks = v.reshape(v.shape[:-1] + (-1, 32))
    amax = np.abs(blocks).max(-1, keepdims=True)
    byte = np.maximum(np.where(amax > 0, np.frexp(amax)[1] - 1 + 127, 0) - down, 1)
    scale = np.exp2(byte - 127.0)
    codes = (blocks / scale).astype(np.float32).astype(dtype).astype(np.float64)
    return np.moveaxis((codes * scale).reshape(v.shape), -1, axis)


WIDE = False


def mx_kscale(k):
    if not WIDE:
        return np.ones(k)
    levels = np.array([30, -30])
    if k % 512:
        return np.exp2(np.random.permutation(np.resize(levels, k // 32))).repeat(32)
    a = np.empty((k // 512, 16))
    for p in range(k // 512):
        a[p, :8] = np.random.permutation(np.resize(levels, 8))
        for g in range(8):
            far = levels[np.abs(levels - a[p, g]) >= 10]
            a[p, g + 8] = far[np.random.randint(len(far))]
    return np.exp2(a.ravel()).repeat(32)


BF16 = ml_dtypes.bfloat16


def bf(x):
    return np.asarray(x, np.float32).astype(BF16)


def f64(x):
    return np.asarray(x).astype(np.float64)


B, S, F, H, D = 2, 256, 2048, 16, 128
THETA = 10000.0
HD = H * D


def rope_tables():
    freqs = 1.0 / THETA ** (f64(np.arange(0, D, 2)) / D)
    ang = np.outer(f64(np.arange(S)), freqs)
    ang = np.concatenate((ang, ang), axis=-1)
    return np.cos(ang), np.sin(ang)


def rotate_half(v):
    v1, v2 = v[..., : D // 2], v[..., D // 2 :]
    return np.concatenate((-v2, v1), axis=-1)


def setup_inputs():
    s = mx_kscale(F)
    return {"x": bf(np.random.standard_normal((B, S, F)) * s),
            "wq": bf(np.random.standard_normal((F, H, D)) / np.sqrt(F) / s[:, None, None]),
            "bq": bf(np.random.standard_normal((H, D)) * 0.3),
            "wk": bf(np.random.standard_normal((F, H, D)) / np.sqrt(F) / s[:, None, None]),
            "bk": bf(np.random.standard_normal((H, D)) * 0.3)}


def reference(x, wq, bq, wk, bk):
    cos, sin = rope_tables()
    cos, sin = cos[None, :, None, :], sin[None, :, None, :]
    xq = mxq(f64(x), 2, "e5m2")
    q = (xq @ mxq(f64(wq).reshape(F, HD), 0, "e5m2")).reshape(B, S, H, D) + f64(bq)
    k = (xq @ mxq(f64(wk).reshape(F, HD), 0, "e5m2")).reshape(B, S, H, D) + f64(bk)
    q_rot = q * cos + rotate_half(q) * sin
    k_rot = k * cos + rotate_half(k) * sin
    return q_rot, k_rot

@@ -1,0 +1,283 @@
+import math
+from contextlib import ExitStack
+
+import concourse.mybir as mybir
+
+B, S, F, H, D = 2, 256, 2048, 16, 128
+THETA = 10000.0
+TOKENS = B * S
+FLOPS = 2 * TOKENS * F * 2 * H * D
+
+F32 = mybir.dt.float32
+BF16 = mybir.dt.bfloat16
+I32 = mybir.dt.int32
+U32 = mybir.dt.uint32
+U8 = mybir.dt.uint8
+E5M2X4 = mybir.dt.float8_e5m2_x4
+ALU = mybir.AluOpType
+ACT = mybir.ActivationFunctionType
+
+P = 128
+PACK = 4
+K_PASS = P * PACK
+PASSES = F // K_PASS
+TOKEN_TILES = TOKENS // P
+HEADS = 2 * H
+PAIRS = HEADS // 2
+PAIR_COLS = 2 * D
+NARROW = 512
+WIDE = 1024
+VECTOR_COLS = 128
+
+
+def tile_selfattention_pa_kernel(tc, x, wq, bq, wk, bk, out_0, out_1):
+    nc = tc.nc
+    x_rows = x.rearrange("b s f -> (b s) f")
+    weights = [w.rearrange("f h d -> f (h d)") for w in (wq, wk)]
+    outs = [o.rearrange("b s h d -> (b s) (h d)") for o in (out_0, out_1)]
+
+    with ExitStack() as ctx:
+        const = ctx.enter_context(tc.tile_pool(name="const", bufs=1))
+        loads = ctx.enter_context(tc.tile_pool(name="loads", bufs=1))
+        work = ctx.enter_context(tc.tile_pool(name="work", bufs=1))
+        psum = ctx.enter_context(tc.psum_pool(name="psum", bufs=4))
+        ctx.enter_context(tc.manual_schedule())
+
+        raw_x = {}
+        raw_w = {}
+
+        def load_x(g):
+            raw_x[g] = loads.tile([P, TOKEN_TILES * K_PASS], BF16, name="narrow", bufs=12)
+            nc.sync.dma_start(
+                out=raw_x[g][:].rearrange("p (t f) -> p t f", t=TOKEN_TILES),
+                in_=x_rows[:, g * K_PASS : (g + 1) * K_PASS].rearrange("(t p) f -> p t f", p=P),
+            )
+
+        def load_w(g, first, width):
+            if width == NARROW:
+                raw = loads.tile([P, PACK, width], BF16, name="narrow", bufs=12)
+            else:
+                raw = loads.tile([P, PACK, width], BF16, name="wide", bufs=8)
+            source = weights[first // (H * D)]
+            col = first % (H * D)
+            nc.sync.dma_start(
+                out=raw[:],
+                in_=source[g * K_PASS : (g + 1) * K_PASS, col : col + width].rearrange("(p j) n -> p j n", j=PACK),
+            )
+            for c in range(0, width, PAIR_COLS):
+                raw_w[(first + c) // PAIR_COLS, g] = raw[:, :, c : c + PAIR_COLS]
+
+        for g in range(PASSES):
+            load_x(g)
+            load_w(g, 0, NARROW)
+        for g in range(PASSES):
+            load_w(g, NARROW, NARROW)
+        for g in range(PASSES):
+            load_w(g, WIDE, WIDE)
+
+        offset = const.tile([P, P], F32, name="offset")
+        nc.gpsimd.iota(offset[:], pattern=[[-1, P]], base=0, channel_multiplier=1, allow_small_or_imprecise_dtypes=True)
+        freq_index = const.tile([P, 1], F32, name="freq_index")
+        for lo in (0, D // 2):
+            nc.gpsimd.iota(freq_index[lo : lo + D // 2, :], pattern=[[0, 1]], base=0, channel_multiplier=1,
+                           allow_small_or_imprecise_dtypes=True)
+        theta = const.tile([P, 1], F32, name="theta")
+        nc.vector.memset(theta[:], THETA)
+        exponent = const.tile([P, 1], F32, name="exponent")
+        nc.gpsimd.tensor_scalar(exponent[:], freq_index[:], -2.0 / D, 0.0, ALU.mult, ALU.add)
+        freq = const.tile([P, 1], F32, name="freq")
+        nc.gpsimd.tensor_tensor(freq[:], theta[:], exponent[:], ALU.pow)
+        position = const.tile([P, S], F32, name="position")
+        nc.gpsimd.iota(position[:], pattern=[[1, S]], base=0, channel_multiplier=0, allow_small_or_imprecise_dtypes=True)
+        bias_rows = const.tile([HEADS, D], BF16, name="bias_rows")
+        nc.gpsimd.dma_start(out=bias_rows[0:H, :], in_=bq)
+        nc.gpsimd.dma_start(out=bias_rows[H:HEADS, :], in_=bk)
+
+        identity = const.tile([P, P], F32, name="identity")
+        nc.vector.tensor_scalar(identity[:], offset[:], 0.0, None, ALU.is_equal)
+        swap = const.tile([P, P], F32, name="swap")
+        nc.vector.tensor_scalar(swap[:, : D // 2], offset[:, : D // 2], float(D // 2), None, ALU.is_equal)
+        nc.vector.tensor_scalar(swap[:, D // 2 :], offset[:, D // 2 :], float(-D // 2), None, ALU.is_equal)
+        bias_square = const.tile([P, P], F32, name="bias_square")
+        nc.vector.memset(bias_square[:], 0.0)
+
+        turn = const.tile([P, 1], F32, name="turn")
+        for lo, sign in ((0, 1.0), (D // 2, -1.0)):
+            nc.vector.tensor_scalar(turn[lo : lo + D // 2, :], freq[lo : lo + D // 2, :], sign / (2 * math.pi), None, ALU.mult)
+        turns = const.tile([P, 2, S], F32, name="turns")
+        for i, shift in enumerate((0.0, -0.25)):
+            nc.vector.tensor_scalar(turns[:, i, :], position[:], turn[:], shift, ALU.mult, ALU.add)
+        whole = const.tile([P, 2, S], I32, name="whole")
+        nc.vector.tensor_copy(whole[:], turns[:])
+        fraction = const.tile([P, 2, S], F32, name="fraction")
+        nc.vector.tensor_tensor(fraction[:], turns[:], whole[:], ALU.subtract)
+        half_sine = const.tile([P, 2, S], F32, name="half_sine")
+        nc.scalar.activation(half_sine[:], fraction[:], ACT.Sin, scale=math.pi)
+        minus_two_squares = const.tile([P, 2, S], F32, name="minus_two_squares")
+        tables = const.tile([P, 2, S], F32, name="tables")
+        bias_cols = const.tile([P, HEADS], F32, name="bias_cols")
+
+        def finish_tables():
+            nc.vector.scalar_tensor_tensor(minus_two_squares[:], half_sine[:], -2.0, half_sine[:], ALU.mult, ALU.mult)
+            nc.vector.tensor_copy(bias_square[0:HEADS, :], bias_rows[:])
+            nc.vector.tensor_scalar(tables[:], minus_two_squares[:], 1.0, None, ALU.add)
+
+        def turn_bias():
+            bank = psum.tile([P, P], F32, name="turned")
+            nc.tensor.transpose(bank[:], bias_square[:], identity[:])
+            nc.scalar.copy(bias_cols[:], bank[:, 0:HEADS])
+
+        x_codes = const.tile([P, PASSES, TOKENS], U32, name="x_codes", align_bytes=64)
+        x_scales = const.tile([P, PASSES, TOKENS], U8, name="x_scales", align_bytes=64)
+        grouped_x = {}
+
+        def turn_x(g):
+            words = raw_x[g][:].bitcast(F32)
+            per_tile = K_PASS // 2
+            grouped_x[g] = work.tile([P, TOKENS * PACK], BF16, name="grouped_x", bufs=2, align_bytes=64)
+            target = grouped_x[g][:].bitcast(F32).rearrange("p (t r u) -> p t r u", t=TOKEN_TILES, u=2)
+            for t0 in range(0, TOKEN_TILES, 2):
+                bank = psum.tile([P, 2, 2, P], F32, name="turned")
+                for t in range(2):
+                    for u in range(2):
+                        start = (t0 + t) * per_tile
+                        nc.tensor.transpose(bank[:, t, u, :], words[:, start + u : start + per_tile : 2], identity[:])
+                nc.scalar.copy(target[:, t0 : t0 + 2, :, :], bank[:].rearrange("p t u r -> p t r u"))
+
+        def quantize_x(g):
+            nc.vector.quantize_mx(out=x_codes[:, g, :].bitcast(E5M2X4), scales=x_scales[:, g, :], in_=grouped_x[g][:])
+
+        grouped_w = {}
+        w_codes = {}
+        w_scales = {}
+
+        def interleave(copy, pair, g, first, last):
+            if pair not in grouped_w:
+                grouped_w[pair] = work.tile([P, PASSES, PAIR_COLS, PACK], BF16, name="grouped_w", bufs=3, align_bytes=64)
+            copy(
+                grouped_w[pair][:, g, first:last, :].rearrange("p (c i) j -> p c j i", i=4),
+                raw_w[pair, g][:, :, first:last].rearrange("p j (c i) -> p c j i", i=4),
+            )
+
+        def quantize_w(pair, first, last):
+            if pair not in w_codes:
+                w_codes[pair] = work.tile([P, PASSES * PAIR_COLS], U32, name="w_codes", bufs=3, align_bytes=64)
+                w_scales[pair] = work.tile([P, PASSES * PAIR_COLS], U8, name="w_scales", bufs=3, align_bytes=64)
+            cols = slice(first * PAIR_COLS, last * PAIR_COLS)
+            nc.vector.quantize_mx(
+                out=w_codes[pair][:, cols].bitcast(E5M2X4),
+                scales=w_scales[pair][:, cols],
+                in_=grouped_w[pair][:, first:last, :, :].rearrange("p g c j -> p (g c j)"),
+            )
+
+        sums = {}
+
+        def multiply(head, g):
+            if g == 0:
+                sums[head] = psum.tile([P, TOKENS], F32, name="sums")
+            pair = head // 2
+            first = g * PAIR_COLS + (head % 2) * D
+            nc.tensor.matmul_mx(
+                out=sums[head][:],
+                lhsT=w_codes[pair][:, first : first + D].bitcast(E5M2X4),
+                lhsT_scale=w_scales[pair][:, first : first + D],
+                rhs=x_codes[:, g, :].bitcast(E5M2X4),
+                rhs_scale=x_scales[:, g, :],
+                start=(g == 0),
+                stop=(g == PASSES - 1),
+            )
+
+        terms = {}
+
+        def weigh(head):
+            terms[head] = work.tile([P, 2, TOKENS], F32, name="terms", bufs=4)
+            for i in range(2):
+                nc.vector.scalar_tensor_tensor(
+                    terms[head][:, i, :].rearrange("p (b s) -> p b s", b=B),
+                    sums[head][:].rearrange("p (b s) -> p b s", b=B),
+                    bias_cols[:, head : head + 1],
+                    tables[:, i : i + 1, :].broadcast_to([P, B, S]),
+                    ALU.add,
+                    ALU.mult,
+                )
+
+        rotated = {}
+
+        def rotate(head):
+            rotated[head] = psum.tile([P, TOKEN_TILES, D], F32, name="turned")
+            for t in range(TOKEN_TILES):
+                for i, order in enumerate((identity, swap)):
+                    nc.tensor.matmul(
+                        rotated[head][:, t, :],
+                        lhsT=terms[head][:, i, t * P : (t + 1) * P],
+                        rhs=order[:],
+                        start=(i == 0),
+                        stop=(i == 1),
+                        is_transpose=True,
+                    )
+
+        staged = {}
+
+        def evacuate(head):
+            pair = head // 2
+            if head % 2 == 0:
+                staged[pair] = work.tile([P, TOKEN_TILES, PAIR_COLS], F32, name="staged", bufs=4)
+            first = (head % 2) * D
+            nc.scalar.copy(staged[pair][:, :, first : first + D], rotated[head][:])
+
+        def store(pair):
+            col = (pair * PAIR_COLS) % (H * D)
+            target = outs[pair * PAIR_COLS // (H * D)][:, col : col + PAIR_COLS]
+            nc.sync.dma_start(out=target.rearrange("(t p) n -> p t n", p=P), in_=staged[pair][:])
+
+        turn_x(0)
+        for g in range(PASSES):
+            interleave(nc.vector.tensor_copy, 0, g, 0, PAIR_COLS)
+            interleave(nc.scalar.copy, 1, g, 0, PAIR_COLS)
+            if g > 0:
+                quantize_w(1, g - 1, g)
+            quantize_x(g)
+            quantize_w(0, g, g + 1)
+            if g == 0:
+                finish_tables()
+            if g + 1 < PASSES:
+                turn_x(g + 1)
+            if g == 1:
+                turn_bias()
+            multiply(0, g)
+            multiply(1, g)
+        quantize_w(1, PASSES - 1, PASSES)
+
+        later_loads = [(g, 2 * WIDE, WIDE) for g in range(PASSES)]
+        later_loads += [(g, 3 * WIDE + c, NARROW) for c in (0, NARROW) for g in range(PASSES)]
+
+        for pair in range(PAIRS):
+            ahead = pair + 2
+            even, odd = 2 * pair, 2 * pair + 1
+            for item in later_loads[2 * pair : 2 * pair + 2]:
+                load_w(*item)
+            if pair > 0:
+                evacuate(even - 1)
+                store(pair - 1)
+            weigh(even)
+            if pair > 0:
+                for g in range(PASSES):
+                    multiply(odd, g)
+            rotate(even)
+            if ahead < PAIRS:
+                interleave(nc.scalar.copy, ahead, 0, 0, PAIR_COLS)
+            if 0 < pair < PAIRS - 1:
+                quantize_w(pair + 1, 0, PASSES)
+            evacuate(even)
+            weigh(odd)
+            if pair < PAIRS - 1:
+                for g in range(PASSES):
+                    multiply(odd + 1, g)
+            rotate(odd)
+            if ahead < PAIRS:
+                interleave(nc.scalar.copy, ahead, 1, 0, PAIR_COLS)
+                interleave(nc.scalar.copy, ahead, 2, 0, PAIR_COLS - VECTOR_COLS)
+                interleave(nc.vector.tensor_copy, ahead, 2, PAIR_COLS - VECTOR_COLS, PAIR_COLS)
+                interleave(nc.vector.tensor_copy, ahead, 3, 0, PAIR_COLS)
+        evacuate(HEADS - 1)
+        store(PAIRS - 1)

@@ -27,7 +27,7 @@ PAIRS = HEADS // 2
 PAIR_COLS = 2 * D
 NARROW = 512
 WIDE = 1024
-VECTOR_COLS = 128
+VECTOR_COLS = 88
 
 
 def tile_selfattention_pa_kernel(tc, x, wq, bq, wk, bk, out_0, out_1):
@@ -43,29 +43,30 @@ def tile_selfattention_pa_kernel(tc, x, wq, bq, wk, bk, out_0, out_1):
         psum = ctx.enter_context(tc.psum_pool(name="psum", bufs=4))
         ctx.enter_context(tc.manual_schedule())
 
-        raw_x = {}
+        raw_x = loads.tile([P, PASSES, TOKEN_TILES * K_PASS], BF16, name="narrow", bufs=3)
         raw_w = {}
 
         def load_x(g):
-            raw_x[g] = loads.tile([P, TOKEN_TILES * K_PASS], BF16, name="narrow", bufs=12)
             nc.sync.dma_start(
-                out=raw_x[g][:].rearrange("p (t f) -> p t f", t=TOKEN_TILES),
+                out=raw_x[:, g, :].rearrange("p (t f) -> p t f", t=TOKEN_TILES),
                 in_=x_rows[:, g * K_PASS : (g + 1) * K_PASS].rearrange("(t p) f -> p t f", p=P),
             )
 
         def load_w(g, first, width):
-            if width == NARROW:
-                raw = loads.tile([P, PACK, width], BF16, name="narrow", bufs=12)
-            else:
-                raw = loads.tile([P, PACK, width], BF16, name="wide", bufs=8)
+            if g == 0:
+                if width == NARROW:
+                    raw = loads.tile([P, PASSES, PACK, width], BF16, name="narrow", bufs=3)
+                else:
+                    raw = loads.tile([P, PASSES, PACK, width], BF16, name="wide", bufs=2)
+                raw_w["tile", first] = raw
+                for c in range(0, width, PAIR_COLS):
+                    raw_w[(first + c) // PAIR_COLS] = raw[:, :, :, c : c + PAIR_COLS]
             source = weights[first // (H * D)]
             col = first % (H * D)
             nc.sync.dma_start(
-                out=raw[:],
+                out=raw_w["tile", first][:, g, :, :],
                 in_=source[g * K_PASS : (g + 1) * K_PASS, col : col + width].rearrange("(p j) n -> p j n", j=PACK),
             )
-            for c in range(0, width, PAIR_COLS):
-                raw_w[(first + c) // PAIR_COLS, g] = raw[:, :, c : c + PAIR_COLS]
 
         for g in range(PASSES):
             load_x(g)
@@ -77,50 +78,41 @@ def tile_selfattention_pa_kernel(tc, x, wq, bq, wk, bk, out_0, out_1):
 
         offset = const.tile([P, P], F32, name="offset")
         nc.gpsimd.iota(offset[:], pattern=[[-1, P]], base=0, channel_multiplier=1, allow_small_or_imprecise_dtypes=True)
-        freq_index = const.tile([P, 1], F32, name="freq_index")
-        for lo in (0, D // 2):
-            nc.gpsimd.iota(freq_index[lo : lo + D // 2, :], pattern=[[0, 1]], base=0, channel_multiplier=1,
-                           allow_small_or_imprecise_dtypes=True)
-        theta = const.tile([P, 1], F32, name="theta")
-        nc.vector.memset(theta[:], THETA)
-        exponent = const.tile([P, 1], F32, name="exponent")
-        nc.gpsimd.tensor_scalar(exponent[:], freq_index[:], -2.0 / D, 0.0, ALU.mult, ALU.add)
-        freq = const.tile([P, 1], F32, name="freq")
-        nc.gpsimd.tensor_tensor(freq[:], theta[:], exponent[:], ALU.pow)
         position = const.tile([P, S], F32, name="position")
         nc.gpsimd.iota(position[:], pattern=[[1, S]], base=0, channel_multiplier=0, allow_small_or_imprecise_dtypes=True)
         bias_rows = const.tile([HEADS, D], BF16, name="bias_rows")
-        nc.gpsimd.dma_start(out=bias_rows[0:H, :], in_=bq)
-        nc.gpsimd.dma_start(out=bias_rows[H:HEADS, :], in_=bk)
+        nc.scalar.dma_start(out=bias_rows[0:H, :], in_=bq)
+        nc.scalar.dma_start(out=bias_rows[H:HEADS, :], in_=bk)
 
+        freq = const.tile([P, 2, D // 2], F32, name="freq")
+        for half, sign in enumerate((1.0, -1.0)):
+            nc.vector.memset(freq[:, half, 0:1], sign)
+        known = 1
+        while known < D // 2:
+            nc.vector.tensor_scalar(freq[:, :, known : 2 * known], freq[:, :, 0:known], THETA ** (-2.0 * known / D), None, ALU.mult)
+            known *= 2
         identity = const.tile([P, P], F32, name="identity")
         nc.vector.tensor_scalar(identity[:], offset[:], 0.0, None, ALU.is_equal)
         swap = const.tile([P, P], F32, name="swap")
         nc.vector.tensor_scalar(swap[:, : D // 2], offset[:, : D // 2], float(D // 2), None, ALU.is_equal)
+        diagonal = const.tile([P, D], F32, name="diagonal")
+        turn = const.tile([P, 1], F32, name="turn")
+        nc.vector.scalar_tensor_tensor(diagonal[:], freq[:].rearrange("p h j -> p (h j)"), 1 / (2 * math.pi), identity[:],
+                                       ALU.mult, ALU.mult, accum_out=turn[:])
         nc.vector.tensor_scalar(swap[:, D // 2 :], offset[:, D // 2 :], float(-D // 2), None, ALU.is_equal)
+        turns = const.tile([P, 2, S], F32, name="turns")
+        for i, shift in enumerate((0.25, 0.0)):
+            nc.vector.tensor_scalar(turns[:, i, :], position[:], turn[:], shift, ALU.mult, ALU.add)
         bias_square = const.tile([P, P], F32, name="bias_square")
         nc.vector.memset(bias_square[:], 0.0)
-
-        turn = const.tile([P, 1], F32, name="turn")
-        for lo, sign in ((0, 1.0), (D // 2, -1.0)):
-            nc.vector.tensor_scalar(turn[lo : lo + D // 2, :], freq[lo : lo + D // 2, :], sign / (2 * math.pi), None, ALU.mult)
-        turns = const.tile([P, 2, S], F32, name="turns")
-        for i, shift in enumerate((0.0, -0.25)):
-            nc.vector.tensor_scalar(turns[:, i, :], position[:], turn[:], shift, ALU.mult, ALU.add)
         whole = const.tile([P, 2, S], I32, name="whole")
         nc.vector.tensor_copy(whole[:], turns[:])
         fraction = const.tile([P, 2, S], F32, name="fraction")
         nc.vector.tensor_tensor(fraction[:], turns[:], whole[:], ALU.subtract)
-        half_sine = const.tile([P, 2, S], F32, name="half_sine")
-        nc.scalar.activation(half_sine[:], fraction[:], ACT.Sin, scale=math.pi)
-        minus_two_squares = const.tile([P, 2, S], F32, name="minus_two_squares")
-        tables = const.tile([P, 2, S], F32, name="tables")
+        tables = const.tile([P, 2, B, S], F32, name="tables")
         bias_cols = const.tile([P, HEADS], F32, name="bias_cols")
-
-        def finish_tables():
-            nc.vector.scalar_tensor_tensor(minus_two_squares[:], half_sine[:], -2.0, half_sine[:], ALU.mult, ALU.mult)
-            nc.vector.tensor_copy(bias_square[0:HEADS, :], bias_rows[:])
-            nc.vector.tensor_scalar(tables[:], minus_two_squares[:], 1.0, None, ALU.add)
+        nc.scalar.activation(tables[:], fraction[:].unsqueeze(2).broadcast_to([P, 2, B, S]), ACT.Sin, scale=2 * math.pi)
+        nc.vector.tensor_copy(bias_square[0:HEADS, :], bias_rows[:])
 
         def turn_bias():
             bank = psum.tile([P, P], F32, name="turned")
@@ -132,7 +124,7 @@ def tile_selfattention_pa_kernel(tc, x, wq, bq, wk, bk, out_0, out_1):
         grouped_x = {}
 
         def turn_x(g):
-            words = raw_x[g][:].bitcast(F32)
+            words = raw_x[:, g, :].bitcast(F32)
             per_tile = K_PASS // 2
             grouped_x[g] = work.tile([P, TOKENS * PACK], BF16, name="grouped_x", bufs=2, align_bytes=64)
             target = grouped_x[g][:].bitcast(F32).rearrange("p (t r u) -> p t r u", t=TOKEN_TILES, u=2)
@@ -151,12 +143,12 @@ def tile_selfattention_pa_kernel(tc, x, wq, bq, wk, bk, out_0, out_1):
         w_codes = {}
         w_scales = {}
 
-        def interleave(copy, pair, g, first, last):
+        def interleave(copy, pair, passes, cols):
             if pair not in grouped_w:
                 grouped_w[pair] = work.tile([P, PASSES, PAIR_COLS, PACK], BF16, name="grouped_w", bufs=3, align_bytes=64)
             copy(
-                grouped_w[pair][:, g, first:last, :].rearrange("p (c i) j -> p c j i", i=4),
-                raw_w[pair, g][:, :, first:last].rearrange("p j (c i) -> p c j i", i=4),
+                grouped_w[pair][:, passes, cols, :].rearrange("p g (c i) j -> p g c j i", i=4),
+                raw_w[pair][:, passes, :, cols].rearrange("p g j (c i) -> p g c j i", i=4),
             )
 
         def quantize_w(pair, first, last):
@@ -189,26 +181,26 @@ def tile_selfattention_pa_kernel(tc, x, wq, bq, wk, bk, out_0, out_1):
 
         terms = {}
 
-        def weigh(head):
-            terms[head] = work.tile([P, 2, TOKENS], F32, name="terms", bufs=4)
-            for i in range(2):
-                nc.vector.scalar_tensor_tensor(
-                    terms[head][:, i, :].rearrange("p (b s) -> p b s", b=B),
-                    sums[head][:].rearrange("p (b s) -> p b s", b=B),
-                    bias_cols[:, head : head + 1],
-                    tables[:, i : i + 1, :].broadcast_to([P, B, S]),
-                    ALU.add,
-                    ALU.mult,
-                )
+        def weigh(head, tokens=slice(0, TOKENS)):
+            if tokens.start == 0:
+                terms[head] = work.tile([P, 2, TOKENS], F32, name="terms", bufs=4)
+            nc.vector.scalar_tensor_tensor(
+                terms[head][:, :, tokens],
+                sums[head][:, tokens].unsqueeze(1).broadcast_to([P, 2, tokens.stop - tokens.start]),
+                bias_cols[:, head : head + 1],
+                tables[:].rearrange("p i b s -> p i (b s)")[:, :, tokens],
+                ALU.add,
+                ALU.mult,
+            )
 
         rotated = {}
 
-        def rotate(head):
-            rotated[head] = psum.tile([P, TOKEN_TILES, D], F32, name="turned")
-            for t in range(TOKEN_TILES):
+        def rotate(head, tiles=slice(0, TOKEN_TILES)):
+            rotated[head, tiles.start] = psum.tile([P, TOKEN_TILES, D], F32, name="turned")
+            for t in range(tiles.start, tiles.stop):
                 for i, order in enumerate((identity, swap)):
                     nc.tensor.matmul(
-                        rotated[head][:, t, :],
+                        rotated[head, tiles.start][:, t, :],
                         lhsT=terms[head][:, i, t * P : (t + 1) * P],
                         rhs=order[:],
                         start=(i == 0),
@@ -218,28 +210,26 @@ def tile_selfattention_pa_kernel(tc, x, wq, bq, wk, bk, out_0, out_1):
 
         staged = {}
 
-        def evacuate(head):
+        def evacuate(head, tiles=slice(0, TOKEN_TILES)):
             pair = head // 2
-            if head % 2 == 0:
+            if pair not in staged:
                 staged[pair] = work.tile([P, TOKEN_TILES, PAIR_COLS], F32, name="staged", bufs=4)
             first = (head % 2) * D
-            nc.scalar.copy(staged[pair][:, :, first : first + D], rotated[head][:])
+            nc.scalar.copy(staged[pair][:, tiles, first : first + D], rotated[head, tiles.start][:, tiles, :])
 
-        def store(pair):
+        def store(pair, cols=slice(0, PAIR_COLS), tiles=slice(0, TOKEN_TILES)):
             col = (pair * PAIR_COLS) % (H * D)
-            target = outs[pair * PAIR_COLS // (H * D)][:, col : col + PAIR_COLS]
-            nc.sync.dma_start(out=target.rearrange("(t p) n -> p t n", p=P), in_=staged[pair][:])
+            target = outs[pair * PAIR_COLS // (H * D)][:, col : col + PAIR_COLS].rearrange("(t p) n -> p t n", p=P)
+            nc.sync.dma_start(out=target[:, tiles, cols], in_=staged[pair][:, tiles, cols])
 
         turn_x(0)
         for g in range(PASSES):
-            interleave(nc.vector.tensor_copy, 0, g, 0, PAIR_COLS)
-            interleave(nc.scalar.copy, 1, g, 0, PAIR_COLS)
+            interleave(nc.vector.tensor_copy, 0, slice(g, g + 1), slice(0, PAIR_COLS))
+            interleave(nc.scalar.copy, 1, slice(g, g + 1), slice(0, PAIR_COLS))
             if g > 0:
                 quantize_w(1, g - 1, g)
             quantize_x(g)
             quantize_w(0, g, g + 1)
-            if g == 0:
-                finish_tables()
             if g + 1 < PASSES:
                 turn_x(g + 1)
             if g == 1:
@@ -251,6 +241,8 @@ def tile_selfattention_pa_kernel(tc, x, wq, bq, wk, bk, out_0, out_1):
         later_loads = [(g, 2 * WIDE, WIDE) for g in range(PASSES)]
         later_loads += [(g, 3 * WIDE + c, NARROW) for c in (0, NARROW) for g in range(PASSES)]
 
+        scalar_cols = slice(0, PAIR_COLS - VECTOR_COLS)
+        vector_cols = slice(PAIR_COLS - VECTOR_COLS, PAIR_COLS)
         for pair in range(PAIRS):
             ahead = pair + 2
             even, odd = 2 * pair, 2 * pair + 1
@@ -265,19 +257,23 @@ def tile_selfattention_pa_kernel(tc, x, wq, bq, wk, bk, out_0, out_1):
                     multiply(odd, g)
             rotate(even)
             if ahead < PAIRS:
-                interleave(nc.scalar.copy, ahead, 0, 0, PAIR_COLS)
+                interleave(nc.scalar.copy, ahead, slice(0, 2), scalar_cols)
             if 0 < pair < PAIRS - 1:
                 quantize_w(pair + 1, 0, PASSES)
             evacuate(even)
+            if pair == PAIRS - 1:
+                break
             weigh(odd)
-            if pair < PAIRS - 1:
-                for g in range(PASSES):
-                    multiply(odd + 1, g)
+            for g in range(PASSES):
+                multiply(odd + 1, g)
             rotate(odd)
             if ahead < PAIRS:
-                interleave(nc.scalar.copy, ahead, 1, 0, PAIR_COLS)
-                interleave(nc.scalar.copy, ahead, 2, 0, PAIR_COLS - VECTOR_COLS)
-                interleave(nc.vector.tensor_copy, ahead, 2, PAIR_COLS - VECTOR_COLS, PAIR_COLS)
-                interleave(nc.vector.tensor_copy, ahead, 3, 0, PAIR_COLS)
-        evacuate(HEADS - 1)
-        store(PAIRS - 1)
+                interleave(nc.scalar.copy, ahead, slice(2, 4), scalar_cols)
+                interleave(nc.vector.tensor_copy, ahead, slice(0, 4), vector_cols)
+        store(PAIRS - 1, cols=slice(0, D))
+        for b in range(B):
+            tiles = slice(2 * b, 2 * b + 2)
+            weigh(HEADS - 1, slice(b * S, (b + 1) * S))
+            rotate(HEADS - 1, tiles)
+            evacuate(HEADS - 1, tiles)
+            store(PAIRS - 1, cols=slice(D, PAIR_COLS), tiles=tiles)

@@ -22,12 +22,16 @@ PACK = 4
 K_PASS = P * PACK
 PASSES = F // K_PASS
 TOKEN_TILES = TOKENS // P
+HALF = D // 2
 HEADS = 2 * H
 PAIRS = HEADS // 2
 PAIR_COLS = 2 * D
-NARROW = 512
-WIDE = 1024
+NARROW = 2 * PAIR_COLS
+WIDE = 4 * PAIR_COLS
 VECTOR_COLS = 88
+VECTOR_COLS_PAIR_1 = 64
+STAGE_HEADS = 4
+STORE_HEADS = (4, 4, 4, 4, 4, 4, 2, 2, 1, 1, 1)
 
 
 def tile_selfattention_pa_kernel(tc, x, wq, bq, wk, bk, out_0, out_1):
@@ -35,6 +39,9 @@ def tile_selfattention_pa_kernel(tc, x, wq, bq, wk, bk, out_0, out_1):
     x_rows = x.rearrange("b s f -> (b s) f")
     weights = [w.rearrange("f h d -> f (h d)") for w in (wq, wk)]
     outs = [o.rearrange("b s h d -> (b s) (h d)") for o in (out_0, out_1)]
+    all_passes = slice(0, PASSES)
+    early_passes, late_passes = slice(0, PASSES // 2), slice(PASSES // 2, PASSES)
+    all_tiles = slice(0, TOKEN_TILES)
 
     with ExitStack() as ctx:
         const = ctx.enter_context(tc.tile_pool(name="const", bufs=1))
@@ -43,79 +50,78 @@ def tile_selfattention_pa_kernel(tc, x, wq, bq, wk, bk, out_0, out_1):
         psum = ctx.enter_context(tc.psum_pool(name="psum", bufs=4))
         ctx.enter_context(tc.manual_schedule())
 
-        raw_x = loads.tile([P, PASSES, TOKEN_TILES * K_PASS], BF16, name="narrow", bufs=3)
-        raw_w = {}
+        raw_x = loads.tile([P, 2, TOKEN_TILES, 2 * K_PASS], BF16, name="narrow", bufs=3)
+        raw_group = {}
+        raw_pair = {}
 
-        def load_x(g):
+        def load_x(i):
             nc.sync.dma_start(
-                out=raw_x[:, g, :].rearrange("p (t f) -> p t f", t=TOKEN_TILES),
-                in_=x_rows[:, g * K_PASS : (g + 1) * K_PASS].rearrange("(t p) f -> p t f", p=P),
+                out=raw_x[:, i, :, :],
+                in_=x_rows[:, 2 * i * K_PASS : 2 * (i + 1) * K_PASS].rearrange("(t p) f -> p t f", p=P),
             )
 
-        def load_w(g, first, width):
+        def load_w(first, g):
+            source, col = divmod(first, H * D)
+            width = (NARROW, WIDE)[source]
             if g == 0:
-                if width == NARROW:
-                    raw = loads.tile([P, PASSES, PACK, width], BF16, name="narrow", bufs=3)
-                else:
-                    raw = loads.tile([P, PASSES, PACK, width], BF16, name="wide", bufs=2)
-                raw_w["tile", first] = raw
+                name, bufs = (("narrow", 3), ("wide", 2))[source]
+                raw_group[first] = loads.tile([P, PASSES, PACK, width], BF16, name=name, bufs=bufs)
                 for c in range(0, width, PAIR_COLS):
-                    raw_w[(first + c) // PAIR_COLS] = raw[:, :, :, c : c + PAIR_COLS]
-            source = weights[first // (H * D)]
-            col = first % (H * D)
-            nc.sync.dma_start(
-                out=raw_w["tile", first][:, g, :, :],
-                in_=source[g * K_PASS : (g + 1) * K_PASS, col : col + width].rearrange("(p j) n -> p j n", j=PACK),
-            )
+                    raw_pair[(first + c) // PAIR_COLS] = raw_group[first][:, :, :, c : c + PAIR_COLS]
+            rows = weights[source][g * K_PASS : (g + 1) * K_PASS, col : col + width]
+            nc.sync.dma_start(out=raw_group[first][:, g, :, :], in_=rows.rearrange("(p j) n -> p j n", j=PACK))
 
         for g in range(PASSES):
-            load_x(g)
-            load_w(g, 0, NARROW)
+            if g % 2 == 0:
+                load_x(g // 2)
+            load_w(0, g)
         for g in range(PASSES):
-            load_w(g, NARROW, NARROW)
-        for g in range(PASSES):
-            load_w(g, WIDE, WIDE)
-
-        offset = const.tile([P, P], F32, name="offset")
-        nc.gpsimd.iota(offset[:], pattern=[[-1, P]], base=0, channel_multiplier=1, allow_small_or_imprecise_dtypes=True)
-        position = const.tile([P, S], F32, name="position")
-        nc.gpsimd.iota(position[:], pattern=[[1, S]], base=0, channel_multiplier=0, allow_small_or_imprecise_dtypes=True)
+            load_w(NARROW, g)
         bias_rows = const.tile([HEADS, D], BF16, name="bias_rows")
         nc.scalar.dma_start(out=bias_rows[0:H, :], in_=bq)
         nc.scalar.dma_start(out=bias_rows[H:HEADS, :], in_=bk)
 
-        freq = const.tile([P, 2, D // 2], F32, name="freq")
+        distance = const.tile([P, P], F32, name="distance")
+        nc.gpsimd.iota(distance[:], pattern=[[-1, P]], base=0, channel_multiplier=1,
+                       allow_small_or_imprecise_dtypes=True)
+        position = const.tile([P, S], F32, name="position")
+        nc.gpsimd.iota(position[:], pattern=[[1, S]], base=0, channel_multiplier=0,
+                       allow_small_or_imprecise_dtypes=True)
+
+        freq = const.tile([P, 2, HALF], F32, name="freq")
         for half, sign in enumerate((1.0, -1.0)):
             nc.vector.memset(freq[:, half, 0:1], sign)
         known = 1
-        while known < D // 2:
-            nc.vector.tensor_scalar(freq[:, :, known : 2 * known], freq[:, :, 0:known], THETA ** (-2.0 * known / D), None, ALU.mult)
+        while known < HALF:
+            nc.vector.tensor_scalar(freq[:, :, known : 2 * known], freq[:, :, 0:known],
+                                    THETA ** (-2.0 * known / D), None, ALU.mult)
             known *= 2
         identity = const.tile([P, P], F32, name="identity")
-        nc.vector.tensor_scalar(identity[:], offset[:], 0.0, None, ALU.is_equal)
+        nc.vector.tensor_scalar(identity[:], distance[:], 0.0, None, ALU.is_equal)
         swap = const.tile([P, P], F32, name="swap")
-        nc.vector.tensor_scalar(swap[:, : D // 2], offset[:, : D // 2], float(D // 2), None, ALU.is_equal)
+        nc.vector.tensor_scalar(swap[:, :HALF], distance[:, :HALF], float(HALF), None, ALU.is_equal)
         diagonal = const.tile([P, D], F32, name="diagonal")
-        turn = const.tile([P, 1], F32, name="turn")
-        nc.vector.scalar_tensor_tensor(diagonal[:], freq[:].rearrange("p h j -> p (h j)"), 1 / (2 * math.pi), identity[:],
-                                       ALU.mult, ALU.mult, accum_out=turn[:])
-        nc.vector.tensor_scalar(swap[:, D // 2 :], offset[:, D // 2 :], float(-D // 2), None, ALU.is_equal)
-        turns = const.tile([P, 2, S], F32, name="turns")
-        for i, shift in enumerate((0.25, 0.0)):
-            nc.vector.tensor_scalar(turns[:, i, :], position[:], turn[:], shift, ALU.mult, ALU.add)
+        turns_per_step = const.tile([P, 1], F32, name="turns_per_step")
+        nc.vector.scalar_tensor_tensor(diagonal[:], freq[:].rearrange("p h c -> p (h c)"), 1 / (2 * math.pi),
+                                       identity[:], ALU.mult, ALU.mult, accum_out=turns_per_step[:])
+        nc.vector.tensor_scalar(swap[:, HALF:], distance[:, HALF:], float(-HALF), None, ALU.is_equal)
         bias_square = const.tile([P, P], F32, name="bias_square")
         nc.vector.memset(bias_square[:], 0.0)
+        turns = const.tile([P, 2, S], F32, name="turns")
+        for i, shift in enumerate((0.25, 0.0)):
+            nc.vector.tensor_scalar(turns[:, i, :], position[:], turns_per_step[:], shift, ALU.mult, ALU.add)
         whole = const.tile([P, 2, S], I32, name="whole")
         nc.vector.tensor_copy(whole[:], turns[:])
         fraction = const.tile([P, 2, S], F32, name="fraction")
         nc.vector.tensor_tensor(fraction[:], turns[:], whole[:], ALU.subtract)
         tables = const.tile([P, 2, B, S], F32, name="tables")
+        nc.scalar.activation(tables[:], fraction[:].unsqueeze(2).broadcast_to([P, 2, B, S]), ACT.Sin,
+                             scale=2 * math.pi)
         bias_cols = const.tile([P, HEADS], F32, name="bias_cols")
-        nc.scalar.activation(tables[:], fraction[:].unsqueeze(2).broadcast_to([P, 2, B, S]), ACT.Sin, scale=2 * math.pi)
-        nc.vector.tensor_copy(bias_square[0:HEADS, :], bias_rows[:])
 
-        def turn_bias():
-            bank = psum.tile([P, P], F32, name="turned")
+        def transpose_bias():
+            nc.vector.tensor_copy(bias_square[0:HEADS, :], bias_rows[:])
+            bank = psum.tile([P, P], F32, name="transposed")
             nc.tensor.transpose(bank[:], bias_square[:], identity[:])
             nc.scalar.copy(bias_cols[:], bank[:, 0:HEADS])
 
@@ -123,21 +129,21 @@ def tile_selfattention_pa_kernel(tc, x, wq, bq, wk, bk, out_0, out_1):
         x_scales = const.tile([P, PASSES, TOKENS], U8, name="x_scales", align_bytes=64)
         grouped_x = {}
 
-        def turn_x(g):
-            words = raw_x[:, g, :].bitcast(F32)
-            per_tile = K_PASS // 2
+        def transpose_x(g):
+            pass_words = K_PASS // 2
+            words = raw_x[:, g // 2, :, :].bitcast(F32)[:, :, (g % 2) * pass_words : (g % 2 + 1) * pass_words]
             grouped_x[g] = work.tile([P, TOKENS * PACK], BF16, name="grouped_x", bufs=2, align_bytes=64)
             target = grouped_x[g][:].bitcast(F32).rearrange("p (t r u) -> p t r u", t=TOKEN_TILES, u=2)
             for t0 in range(0, TOKEN_TILES, 2):
-                bank = psum.tile([P, 2, 2, P], F32, name="turned")
+                bank = psum.tile([P, 2, 2, P], F32, name="transposed")
                 for t in range(2):
                     for u in range(2):
-                        start = (t0 + t) * per_tile
-                        nc.tensor.transpose(bank[:, t, u, :], words[:, start + u : start + per_tile : 2], identity[:])
+                        nc.tensor.transpose(bank[:, t, u, :], words[:, t0 + t, u:pass_words:2], identity[:])
                 nc.scalar.copy(target[:, t0 : t0 + 2, :, :], bank[:].rearrange("p t u r -> p t r u"))
 
         def quantize_x(g):
-            nc.vector.quantize_mx(out=x_codes[:, g, :].bitcast(E5M2X4), scales=x_scales[:, g, :], in_=grouped_x[g][:])
+            nc.vector.quantize_mx(out=x_codes[:, g, :].bitcast(E5M2X4), scales=x_scales[:, g, :],
+                                  in_=grouped_x[g][:])
 
         grouped_w = {}
         w_codes = {}
@@ -145,45 +151,54 @@ def tile_selfattention_pa_kernel(tc, x, wq, bq, wk, bk, out_0, out_1):
 
         def interleave(copy, pair, passes, cols):
             if pair not in grouped_w:
-                grouped_w[pair] = work.tile([P, PASSES, PAIR_COLS, PACK], BF16, name="grouped_w", bufs=3, align_bytes=64)
+                grouped_w[pair] = work.tile([P, PASSES, PAIR_COLS, PACK], BF16, name="grouped_w", bufs=3,
+                                            align_bytes=64)
             copy(
                 grouped_w[pair][:, passes, cols, :].rearrange("p g (c i) j -> p g c j i", i=4),
-                raw_w[pair][:, passes, :, cols].rearrange("p g j (c i) -> p g c j i", i=4),
+                raw_pair[pair][:, passes, :, cols].rearrange("p g j (c i) -> p g c j i", i=4),
             )
 
-        def quantize_w(pair, first, last):
+        def interleave_on_scalar(pair, passes, vector_cols=VECTOR_COLS):
+            interleave(nc.scalar.copy, pair, passes, slice(0, PAIR_COLS - vector_cols))
+
+        def interleave_on_vector(pair, passes, vector_cols=VECTOR_COLS):
+            interleave(nc.vector.tensor_copy, pair, passes, slice(PAIR_COLS - vector_cols, PAIR_COLS))
+
+        def quantize_w(pair, passes):
             if pair not in w_codes:
                 w_codes[pair] = work.tile([P, PASSES * PAIR_COLS], U32, name="w_codes", bufs=3, align_bytes=64)
                 w_scales[pair] = work.tile([P, PASSES * PAIR_COLS], U8, name="w_scales", bufs=3, align_bytes=64)
-            cols = slice(first * PAIR_COLS, last * PAIR_COLS)
+            cols = slice(passes.start * PAIR_COLS, passes.stop * PAIR_COLS)
             nc.vector.quantize_mx(
                 out=w_codes[pair][:, cols].bitcast(E5M2X4),
                 scales=w_scales[pair][:, cols],
-                in_=grouped_w[pair][:, first:last, :, :].rearrange("p g c j -> p (g c j)"),
+                in_=grouped_w[pair][:, passes, :, :].rearrange("p g c j -> p (g c j)"),
             )
 
         sums = {}
-
-        def multiply(head, g):
-            if g == 0:
-                sums[head] = psum.tile([P, TOKENS], F32, name="sums")
-            pair = head // 2
-            first = g * PAIR_COLS + (head % 2) * D
-            nc.tensor.matmul_mx(
-                out=sums[head][:],
-                lhsT=w_codes[pair][:, first : first + D].bitcast(E5M2X4),
-                lhsT_scale=w_scales[pair][:, first : first + D],
-                rhs=x_codes[:, g, :].bitcast(E5M2X4),
-                rhs_scale=x_scales[:, g, :],
-                start=(g == 0),
-                stop=(g == PASSES - 1),
-            )
-
         terms = {}
+        rotated = {}
+        staged = {}
 
-        def weigh(head, tokens=slice(0, TOKENS)):
-            if tokens.start == 0:
+        def multiply(head, passes=all_passes):
+            if passes.start == 0:
+                sums[head] = psum.tile([P, TOKENS], F32, name="sums")
+            for g in range(passes.start, passes.stop):
+                first = g * PAIR_COLS + (head % 2) * D
+                nc.tensor.matmul_mx(
+                    out=sums[head][:],
+                    lhsT=w_codes[head // 2][:, first : first + D].bitcast(E5M2X4),
+                    lhsT_scale=w_scales[head // 2][:, first : first + D],
+                    rhs=x_codes[:, g, :].bitcast(E5M2X4),
+                    rhs_scale=x_scales[:, g, :],
+                    start=(g == 0),
+                    stop=(g == PASSES - 1),
+                )
+
+        def weigh(head, tiles=all_tiles):
+            if tiles.start == 0:
                 terms[head] = work.tile([P, 2, TOKENS], F32, name="terms", bufs=4)
+            tokens = slice(tiles.start * P, tiles.stop * P)
             nc.vector.scalar_tensor_tensor(
                 terms[head][:, :, tokens],
                 sums[head][:, tokens].unsqueeze(1).broadcast_to([P, 2, tokens.stop - tokens.start]),
@@ -193,14 +208,12 @@ def tile_selfattention_pa_kernel(tc, x, wq, bq, wk, bk, out_0, out_1):
                 ALU.mult,
             )
 
-        rotated = {}
-
-        def rotate(head, tiles=slice(0, TOKEN_TILES)):
-            rotated[head, tiles.start] = psum.tile([P, TOKEN_TILES, D], F32, name="turned")
+        def rotate(head, tiles=all_tiles):
+            rotated[head] = psum.tile([P, TOKEN_TILES, D], F32, name="transposed")
             for t in range(tiles.start, tiles.stop):
                 for i, order in enumerate((identity, swap)):
                     nc.tensor.matmul(
-                        rotated[head, tiles.start][:, t, :],
+                        rotated[head][:, t, :],
                         lhsT=terms[head][:, i, t * P : (t + 1) * P],
                         rhs=order[:],
                         start=(i == 0),
@@ -208,72 +221,81 @@ def tile_selfattention_pa_kernel(tc, x, wq, bq, wk, bk, out_0, out_1):
                         is_transpose=True,
                     )
 
-        staged = {}
+        def evacuate(head, tiles=all_tiles):
+            stage, place = divmod(head, STAGE_HEADS)
+            if stage not in staged:
+                staged[stage] = work.tile([P, TOKEN_TILES, STAGE_HEADS * D], F32, name="staged", bufs=3)
+            nc.scalar.copy(staged[stage][:, tiles, place * D : (place + 1) * D], rotated[head][:, tiles, :])
 
-        def evacuate(head, tiles=slice(0, TOKEN_TILES)):
-            pair = head // 2
-            if pair not in staged:
-                staged[pair] = work.tile([P, TOKEN_TILES, PAIR_COLS], F32, name="staged", bufs=4)
-            first = (head % 2) * D
-            nc.scalar.copy(staged[pair][:, tiles, first : first + D], rotated[head, tiles.start][:, tiles, :])
+        def store(first_head, count, tiles=all_tiles):
+            stage, place = divmod(first_head, STAGE_HEADS)
+            col = (first_head % H) * D
+            target = outs[first_head // H][:, col : col + count * D].rearrange("(t p) n -> p t n", p=P)
+            nc.sync.dma_start(out=target[:, tiles, :], in_=staged[stage][:, tiles, place * D : (place + count) * D])
 
-        def store(pair, cols=slice(0, PAIR_COLS), tiles=slice(0, TOKEN_TILES)):
-            col = (pair * PAIR_COLS) % (H * D)
-            target = outs[pair * PAIR_COLS // (H * D)][:, col : col + PAIR_COLS].rearrange("(t p) n -> p t n", p=P)
-            nc.sync.dma_start(out=target[:, tiles, cols], in_=staged[pair][:, tiles, cols])
+        store_after = {sum(STORE_HEADS[: n + 1]) - 1: count for n, count in enumerate(STORE_HEADS)}
 
-        turn_x(0)
+        def ship(head):
+            evacuate(head)
+            if head in store_after:
+                store(head + 1 - store_after[head], store_after[head])
+
+        transpose_x(0)
         for g in range(PASSES):
-            interleave(nc.vector.tensor_copy, 0, slice(g, g + 1), slice(0, PAIR_COLS))
-            interleave(nc.scalar.copy, 1, slice(g, g + 1), slice(0, PAIR_COLS))
+            one_pass = slice(g, g + 1)
+            interleave_on_vector(0, one_pass, PAIR_COLS)
+            interleave_on_vector(1, one_pass, VECTOR_COLS_PAIR_1)
+            interleave_on_scalar(1, one_pass, VECTOR_COLS_PAIR_1)
             if g > 0:
-                quantize_w(1, g - 1, g)
+                quantize_w(1, slice(g - 1, g))
             quantize_x(g)
-            quantize_w(0, g, g + 1)
+            quantize_w(0, one_pass)
             if g + 1 < PASSES:
-                turn_x(g + 1)
+                transpose_x(g + 1)
             if g == 1:
-                turn_bias()
-            multiply(0, g)
-            multiply(1, g)
-        quantize_w(1, PASSES - 1, PASSES)
-
-        later_loads = [(g, 2 * WIDE, WIDE) for g in range(PASSES)]
-        later_loads += [(g, 3 * WIDE + c, NARROW) for c in (0, NARROW) for g in range(PASSES)]
-
-        scalar_cols = slice(0, PAIR_COLS - VECTOR_COLS)
-        vector_cols = slice(PAIR_COLS - VECTOR_COLS, PAIR_COLS)
-        for pair in range(PAIRS):
-            ahead = pair + 2
-            even, odd = 2 * pair, 2 * pair + 1
-            for item in later_loads[2 * pair : 2 * pair + 2]:
-                load_w(*item)
-            if pair > 0:
-                evacuate(even - 1)
-                store(pair - 1)
-            weigh(even)
-            if pair > 0:
-                for g in range(PASSES):
-                    multiply(odd, g)
-            rotate(even)
-            if ahead < PAIRS:
-                interleave(nc.scalar.copy, ahead, slice(0, 2), scalar_cols)
-            if 0 < pair < PAIRS - 1:
-                quantize_w(pair + 1, 0, PASSES)
-            evacuate(even)
-            if pair == PAIRS - 1:
-                break
-            weigh(odd)
+                transpose_bias()
+            multiply(0, one_pass)
+            multiply(1, one_pass)
+        quantize_w(1, slice(PASSES - 1, PASSES))
+        for first in range(2 * NARROW, H * D, NARROW):
             for g in range(PASSES):
-                multiply(odd + 1, g)
+                load_w(first, g)
+        multiply(2)
+        multiply(3)
+        for head in (0, 1):
+            weigh(head)
+            rotate(head)
+        interleave_on_scalar(2, early_passes)
+
+        wk_loads = [(first, g) for first in range(H * D, 2 * H * D, WIDE) for g in range(PASSES)]
+        for pair in range(1, PAIRS - 1):
+            even, odd = 2 * pair, 2 * pair + 1
+            if pair <= len(wk_loads):
+                load_w(*wk_loads[pair - 1])
+            interleave_on_scalar(pair + 1, late_passes)
+            interleave_on_vector(pair + 1, all_passes)
+            for head in range(max(even - 3, 0), even - 1):
+                ship(head)
+            weigh(even)
+            rotate(even)
+            quantize_w(pair + 1, early_passes)
+            quantize_w(pair + 1, late_passes)
+            weigh(odd)
+            multiply(even + 2)
+            multiply(odd + 2)
             rotate(odd)
-            if ahead < PAIRS:
-                interleave(nc.scalar.copy, ahead, slice(2, 4), scalar_cols)
-                interleave(nc.vector.tensor_copy, ahead, slice(0, 4), vector_cols)
-        store(PAIRS - 1, cols=slice(0, D))
-        for b in range(B):
-            tiles = slice(2 * b, 2 * b + 2)
-            weigh(HEADS - 1, slice(b * S, (b + 1) * S))
-            rotate(HEADS - 1, tiles)
-            evacuate(HEADS - 1, tiles)
-            store(PAIRS - 1, cols=slice(D, PAIR_COLS), tiles=tiles)
+            if pair + 2 < PAIRS:
+                interleave_on_scalar(pair + 2, early_passes)
+
+        last = HEADS - 1
+        ship(last - 4)
+        ship(last - 3)
+        weigh(last - 1)
+        rotate(last - 1)
+        ship(last - 2)
+        ship(last - 1)
+        for tiles in (slice(0, TOKEN_TILES // 2), slice(TOKEN_TILES // 2, TOKEN_TILES)):
+            weigh(last, tiles)
+            rotate(last, tiles)
+            evacuate(last, tiles)
+            store(last, 1, tiles)

@@ -28,7 +28,7 @@ PAIRS = HEADS // 2
 PAIR_COLS = 2 * D
 NARROW = 2 * PAIR_COLS
 WIDE = 4 * PAIR_COLS
-VECTOR_COLS = 88
+VECTOR_COLS = 76
 VECTOR_COLS_PAIR_1 = 64
 STAGE_HEADS = 4
 STORE_HEADS = (4, 4, 4, 4, 4, 4, 2, 2, 1, 1, 1)

import math
from contextlib import ExitStack

import concourse.mybir as mybir

B, S, F, H, D = 2, 256, 2048, 16, 128
THETA = 10000.0
TOKENS = B * S
FLOPS = 2 * TOKENS * F * 2 * H * D

F32 = mybir.dt.float32
BF16 = mybir.dt.bfloat16
I32 = mybir.dt.int32
U32 = mybir.dt.uint32
U8 = mybir.dt.uint8
E5M2X4 = mybir.dt.float8_e5m2_x4
ALU = mybir.AluOpType
ACT = mybir.ActivationFunctionType

P = 128
PACK = 4
K_PASS = P * PACK
PASSES = F // K_PASS
TOKEN_TILES = TOKENS // P
HALF = D // 2
HEADS = 2 * H
PAIRS = HEADS // 2
PAIR_COLS = 2 * D
NARROW = 2 * PAIR_COLS
WIDE = 4 * PAIR_COLS
VECTOR_COLS = 76
VECTOR_COLS_PAIR_1 = 64
STAGE_HEADS = 4
STORE_HEADS = (4, 4, 4, 4, 4, 4, 2, 2, 1, 1, 1)


def tile_selfattention_pa_kernel(tc, x, wq, bq, wk, bk, out_0, out_1):
    nc = tc.nc
    x_rows = x.rearrange("b s f -> (b s) f")
    weights = [w.rearrange("f h d -> f (h d)") for w in (wq, wk)]
    outs = [o.rearrange("b s h d -> (b s) (h d)") for o in (out_0, out_1)]
    all_passes = slice(0, PASSES)
    early_passes, late_passes = slice(0, PASSES // 2), slice(PASSES // 2, PASSES)
    all_tiles = slice(0, TOKEN_TILES)

    with ExitStack() as ctx:
        const = ctx.enter_context(tc.tile_pool(name="const", bufs=1))
        loads = ctx.enter_context(tc.tile_pool(name="loads", bufs=1))
        work = ctx.enter_context(tc.tile_pool(name="work", bufs=1))
        psum = ctx.enter_context(tc.psum_pool(name="psum", bufs=4))
        ctx.enter_context(tc.manual_schedule())

        raw_x = loads.tile([P, 2, TOKEN_TILES, 2 * K_PASS], BF16, name="narrow", bufs=3)
        raw_group = {}
        raw_pair = {}

        def load_x(i):
            nc.sync.dma_start(
                out=raw_x[:, i, :, :],
                in_=x_rows[:, 2 * i * K_PASS : 2 * (i + 1) * K_PASS].rearrange("(t p) f -> p t f", p=P),
            )

        def load_w(first, g):
            source, col = divmod(first, H * D)
            width = (NARROW, WIDE)[source]
            if g == 0:
                name, bufs = (("narrow", 3), ("wide", 2))[source]
                raw_group[first] = loads.tile([P, PASSES, PACK, width], BF16, name=name, bufs=bufs)
                for c in range(0, width, PAIR_COLS):
                    raw_pair[(first + c) // PAIR_COLS] = raw_group[first][:, :, :, c : c + PAIR_COLS]
            rows = weights[source][g * K_PASS : (g + 1) * K_PASS, col : col + width]
            nc.sync.dma_start(out=raw_group[first][:, g, :, :], in_=rows.rearrange("(p j) n -> p j n", j=PACK))

        for g in range(PASSES):
            if g % 2 == 0:
                load_x(g // 2)
            load_w(0, g)
        for g in range(PASSES):
            load_w(NARROW, g)
        bias_rows = const.tile([HEADS, D], BF16, name="bias_rows")
        nc.scalar.dma_start(out=bias_rows[0:H, :], in_=bq)
        nc.scalar.dma_start(out=bias_rows[H:HEADS, :], in_=bk)

        distance = const.tile([P, P], F32, name="distance")
        nc.gpsimd.iota(distance[:], pattern=[[-1, P]], base=0, channel_multiplier=1,
                       allow_small_or_imprecise_dtypes=True)
        position = const.tile([P, S], F32, name="position")
        nc.gpsimd.iota(position[:], pattern=[[1, S]], base=0, channel_multiplier=0,
                       allow_small_or_imprecise_dtypes=True)

        freq = const.tile([P, 2, HALF], F32, name="freq")
        for half, sign in enumerate((1.0, -1.0)):
            nc.vector.memset(freq[:, half, 0:1], sign)
        known = 1
        while known < HALF:
            nc.vector.tensor_scalar(freq[:, :, known : 2 * known], freq[:, :, 0:known],
                                    THETA ** (-2.0 * known / D), None, ALU.mult)
            known *= 2
        identity = const.tile([P, P], F32, name="identity")
        nc.vector.tensor_scalar(identity[:], distance[:], 0.0, None, ALU.is_equal)
        swap = const.tile([P, P], F32, name="swap")
        nc.vector.tensor_scalar(swap[:, :HALF], distance[:, :HALF], float(HALF), None, ALU.is_equal)
        diagonal = const.tile([P, D], F32, name="diagonal")
        turns_per_step = const.tile([P, 1], F32, name="turns_per_step")
        nc.vector.scalar_tensor_tensor(diagonal[:], freq[:].rearrange("p h c -> p (h c)"), 1 / (2 * math.pi),
                                       identity[:], ALU.mult, ALU.mult, accum_out=turns_per_step[:])
        nc.vector.tensor_scalar(swap[:, HALF:], distance[:, HALF:], float(-HALF), None, ALU.is_equal)
        bias_square = const.tile([P, P], F32, name="bias_square")
        nc.vector.memset(bias_square[:], 0.0)
        turns = const.tile([P, 2, S], F32, name="turns")
        for i, shift in enumerate((0.25, 0.0)):
            nc.vector.tensor_scalar(turns[:, i, :], position[:], turns_per_step[:], shift, ALU.mult, ALU.add)
        whole = const.tile([P, 2, S], I32, name="whole")
        nc.vector.tensor_copy(whole[:], turns[:])
        fraction = const.tile([P, 2, S], F32, name="fraction")
        nc.vector.tensor_tensor(fraction[:], turns[:], whole[:], ALU.subtract)
        tables = const.tile([P, 2, B, S], F32, name="tables")
        nc.scalar.activation(tables[:], fraction[:].unsqueeze(2).broadcast_to([P, 2, B, S]), ACT.Sin,
                             scale=2 * math.pi)
        bias_cols = const.tile([P, HEADS], F32, name="bias_cols")

        def transpose_bias():
            nc.vector.tensor_copy(bias_square[0:HEADS, :], bias_rows[:])
            bank = psum.tile([P, P], F32, name="transposed")
            nc.tensor.transpose(bank[:], bias_square[:], identity[:])
            nc.scalar.copy(bias_cols[:], bank[:, 0:HEADS])

        x_codes = const.tile([P, PASSES, TOKENS], U32, name="x_codes", align_bytes=64)
        x_scales = const.tile([P, PASSES, TOKENS], U8, name="x_scales", align_bytes=64)
        grouped_x = {}

        def transpose_x(g):
            pass_words = K_PASS // 2
            words = raw_x[:, g // 2, :, :].bitcast(F32)[:, :, (g % 2) * pass_words : (g % 2 + 1) * pass_words]
            grouped_x[g] = work.tile([P, TOKENS * PACK], BF16, name="grouped_x", bufs=2, align_bytes=64)
            target = grouped_x[g][:].bitcast(F32).rearrange("p (t r u) -> p t r u", t=TOKEN_TILES, u=2)
            for t0 in range(0, TOKEN_TILES, 2):
                bank = psum.tile([P, 2, 2, P], F32, name="transposed")
                for t in range(2):
                    for u in range(2):
                        nc.tensor.transpose(bank[:, t, u, :], words[:, t0 + t, u:pass_words:2], identity[:])
                nc.scalar.copy(target[:, t0 : t0 + 2, :, :], bank[:].rearrange("p t u r -> p t r u"))

        def quantize_x(g):
            nc.vector.quantize_mx(out=x_codes[:, g, :].bitcast(E5M2X4), scales=x_scales[:, g, :],
                                  in_=grouped_x[g][:])

        grouped_w = {}
        w_codes = {}
        w_scales = {}

        def interleave(copy, pair, passes, cols):
            if pair not in grouped_w:
                grouped_w[pair] = work.tile([P, PASSES, PAIR_COLS, PACK], BF16, name="grouped_w", bufs=3,
                                            align_bytes=64)
            copy(
                grouped_w[pair][:, passes, cols, :].rearrange("p g (c i) j -> p g c j i", i=4),
                raw_pair[pair][:, passes, :, cols].rearrange("p g j (c i) -> p g c j i", i=4),
            )

        def interleave_on_scalar(pair, passes, vector_cols=VECTOR_COLS):
            interleave(nc.scalar.copy, pair, passes, slice(0, PAIR_COLS - vector_cols))

        def interleave_on_vector(pair, passes, vector_cols=VECTOR_COLS):
            interleave(nc.vector.tensor_copy, pair, passes, slice(PAIR_COLS - vector_cols, PAIR_COLS))

        def quantize_w(pair, passes):
            if pair not in w_codes:
                w_codes[pair] = work.tile([P, PASSES * PAIR_COLS], U32, name="w_codes", bufs=3, align_bytes=64)
                w_scales[pair] = work.tile([P, PASSES * PAIR_COLS], U8, name="w_scales", bufs=3, align_bytes=64)
            cols = slice(passes.start * PAIR_COLS, passes.stop * PAIR_COLS)
            nc.vector.quantize_mx(
                out=w_codes[pair][:, cols].bitcast(E5M2X4),
                scales=w_scales[pair][:, cols],
                in_=grouped_w[pair][:, passes, :, :].rearrange("p g c j -> p (g c j)"),
            )

        sums = {}
        terms = {}
        rotated = {}
        staged = {}

        def multiply(head, passes=all_passes):
            if passes.start == 0:
                sums[head] = psum.tile([P, TOKENS], F32, name="sums")
            for g in range(passes.start, passes.stop):
                first = g * PAIR_COLS + (head % 2) * D
                nc.tensor.matmul_mx(
                    out=sums[head][:],
                    lhsT=w_codes[head // 2][:, first : first + D].bitcast(E5M2X4),
                    lhsT_scale=w_scales[head // 2][:, first : first + D],
                    rhs=x_codes[:, g, :].bitcast(E5M2X4),
                    rhs_scale=x_scales[:, g, :],
                    start=(g == 0),
                    stop=(g == PASSES - 1),
                )

        def weigh(head, tiles=all_tiles):
            if tiles.start == 0:
                terms[head] = work.tile([P, 2, TOKENS], F32, name="terms", bufs=4)
            tokens = slice(tiles.start * P, tiles.stop * P)
            nc.vector.scalar_tensor_tensor(
                terms[head][:, :, tokens],
                sums[head][:, tokens].unsqueeze(1).broadcast_to([P, 2, tokens.stop - tokens.start]),
                bias_cols[:, head : head + 1],
                tables[:].rearrange("p i b s -> p i (b s)")[:, :, tokens],
                ALU.add,
                ALU.mult,
            )

        def rotate(head, tiles=all_tiles):
            rotated[head] = psum.tile([P, TOKEN_TILES, D], F32, name="transposed")
            for t in range(tiles.start, tiles.stop):
                for i, order in enumerate((identity, swap)):
                    nc.tensor.matmul(
                        rotated[head][:, t, :],
                        lhsT=terms[head][:, i, t * P : (t + 1) * P],
                        rhs=order[:],
                        start=(i == 0),
                        stop=(i == 1),
                        is_transpose=True,
                    )

        def evacuate(head, tiles=all_tiles):
            stage, place = divmod(head, STAGE_HEADS)
            if stage not in staged:
                staged[stage] = work.tile([P, TOKEN_TILES, STAGE_HEADS * D], F32, name="staged", bufs=3)
            nc.scalar.copy(staged[stage][:, tiles, place * D : (place + 1) * D], rotated[head][:, tiles, :])

        def store(first_head, count, tiles=all_tiles):
            stage, place = divmod(first_head, STAGE_HEADS)
            col = (first_head % H) * D
            target = outs[first_head // H][:, col : col + count * D].rearrange("(t p) n -> p t n", p=P)
            nc.sync.dma_start(out=target[:, tiles, :], in_=staged[stage][:, tiles, place * D : (place + count) * D])

        store_after = {sum(STORE_HEADS[: n + 1]) - 1: count for n, count in enumerate(STORE_HEADS)}

        def ship(head):
            evacuate(head)
            if head in store_after:
                store(head + 1 - store_after[head], store_after[head])

        transpose_x(0)
        for g in range(PASSES):
            one_pass = slice(g, g + 1)
            interleave_on_vector(0, one_pass, PAIR_COLS)
            interleave_on_vector(1, one_pass, VECTOR_COLS_PAIR_1)
            interleave_on_scalar(1, one_pass, VECTOR_COLS_PAIR_1)
            if g > 0:
                quantize_w(1, slice(g - 1, g))
            quantize_x(g)
            quantize_w(0, one_pass)
            if g + 1 < PASSES:
                transpose_x(g + 1)
            if g == 1:
                transpose_bias()
            multiply(0, one_pass)
            multiply(1, one_pass)
        quantize_w(1, slice(PASSES - 1, PASSES))
        for first in range(2 * NARROW, H * D, NARROW):
            for g in range(PASSES):
                load_w(first, g)
        multiply(2)
        multiply(3)
        for head in (0, 1):
            weigh(head)
            rotate(head)
        interleave_on_scalar(2, early_passes)

        wk_loads = [(first, g) for first in range(H * D, 2 * H * D, WIDE) for g in range(PASSES)]
        for pair in range(1, PAIRS - 1):
            even, odd = 2 * pair, 2 * pair + 1
            if pair <= len(wk_loads):
                load_w(*wk_loads[pair - 1])
            interleave_on_scalar(pair + 1, late_passes)
            interleave_on_vector(pair + 1, all_passes)
            for head in range(max(even - 3, 0), even - 1):
                ship(head)
            weigh(even)
            rotate(even)
            quantize_w(pair + 1, early_passes)
            quantize_w(pair + 1, late_passes)
            weigh(odd)
            multiply(even + 2)
            multiply(odd + 2)
            rotate(odd)
            if pair + 2 < PAIRS:
                interleave_on_scalar(pair + 2, early_passes)

        last = HEADS - 1
        ship(last - 4)
        ship(last - 3)
        weigh(last - 1)
        rotate(last - 1)
        ship(last - 2)
        ship(last - 1)
        for tiles in (slice(0, TOKEN_TILES // 2), slice(TOKEN_TILES // 2, TOKEN_TILES)):
            weigh(last, tiles)
            rotate(last, tiles)
            evacuate(last, tiles)
            store(last, 1, tiles)
